import numpy as np
import ml_dtypes


def mxq(x, axis, fmt="e4m3"):
    dtype, down = {"e4m3": (ml_dtypes.float8_e4m3fn, 7), "e5m2": (ml_dtypes.float8_e5m2, 14)}[fmt]
    v = np.moveaxis(np.asarray(x, np.float32).astype(ml_dtypes.bfloat16).astype(np.float64), axis, -1)
    blocks = v.reshape(v.shape[:-1] + (-1, 32))
    amax = np.abs(blocks).max(-1, keepdims=True)
    byte = np.maximum(np.where(amax > 0, np.frexp(amax)[1] - 1 + 127, 0) - down, 1)
    scale = np.exp2(byte - 127.0)
    codes = (blocks / scale).astype(np.float32).astype(dtype).astype(np.float64)
    return np.moveaxis((codes * scale).reshape(v.shape), -1, axis)


WIDE = False


def mx_kscale(k):
    if not WIDE:
        return np.ones(k)
    levels = np.array([10, -10, 5, -5, 0])
    a = np.random.permutation(np.resize(levels, k // 512 * 4)).reshape(k // 512, 4)
    idx = np.arange(k)
    return np.exp2(a[idx // 512, idx % 128 // 32])


BF16 = ml_dtypes.bfloat16


def bf(x):
    return np.asarray(x, np.float32).astype(BF16)


def f64(x):
    return np.asarray(x).astype(np.float64)


B, I, O, C, L = 8, 1024, 128, 4, 8
EDGES = min(L * int(np.lcm(I, O)), I * O)
KO = EDGES // O
KI = EDGES // I
SIGN = 1


def make_mask():
    cols = np.repeat(np.arange(I), KI)
    np.random.shuffle(cols)
    cols = cols.reshape(O, KO)
    m = np.zeros((O, I))
    m[np.arange(O)[:, None], cols] = 1.0
    return m


def setup_inputs():
    s = mx_kscale(I)
    g = np.exp2(np.round(np.log2(s.mean())))
    a = np.random.standard_normal((B, I, I))
    a[:, np.arange(I), np.arange(I)] *= 8.0
    a = a * (KO / 4.0) * (g * g) / s[:, None] / s[None, :]
    return {"input": bf(a), "mask": bf(make_mask()), "weight": bf(np.random.random_sample((C, O, I)) * (3.0 / KO) * s)}


def reference(input, mask, weight):
    compressor = f64(mask) * f64(weight)
    inp = f64(input)
    inp = inp * (1.0 - np.eye(inp.shape[-1]))
    cq = mxq(compressor, 2, "e4m3")
    tmp = cq[None] @ mxq(inp, 1, "e4m3")[:, None]
    out = mxq(tmp, 3, "e4m3") @ cq.transpose(0, 2, 1)[None]
    rs = compressor.sum(-1)
    norm = rs[:, :, None] * rs[:, None, :]
    out = out / np.where(norm == 0, np.ones_like(norm), norm)
    out = SIGN * out
    return out.reshape(B * C, O, O)

@@ -1,0 +1,247 @@
+from contextlib import ExitStack
+
+import concourse.mybir as mybir
+from concourse.masks import make_identity
+
+F32 = mybir.dt.float32
+BF16 = mybir.dt.bfloat16
+U32 = mybir.dt.uint32
+U8 = mybir.dt.uint8
+FP8X4 = mybir.dt.float8_e4m3fn_x4
+ALU = mybir.AluOpType
+ACT = mybir.ActivationFunctionType
+
+P = 128
+B, I, O, C = 8, 1024, 128, 4
+NCH = 2 * B
+FLOPS = 2 * B * C * O * I * I + 2 * B * C * O * I * O
+
+PIN = False
+VCOLS = 640
+AHEAD = 6
+
+
+def tile_verticalcompression_t_kernel(tc, a_in, mask, weight, out):
+    nc = tc.nc
+    with ExitStack() as ctx:
+        const = ctx.enter_context(tc.tile_pool(name="const", bufs=1))
+        rawp = ctx.enter_context(tc.tile_pool(name="rawp", bufs=AHEAD))
+        grpp = ctx.enter_context(tc.tile_pool(name="grpp", bufs=4))
+        acp = ctx.enter_context(tc.tile_pool(name="acp", bufs=6))
+        tgp = ctx.enter_context(tc.tile_pool(name="tgp", bufs=2))
+        outp = ctx.enter_context(tc.tile_pool(name="outp", bufs=3))
+        ps1 = ctx.enter_context(tc.psum_pool(name="ps1", bufs=6))
+        ps2 = ctx.enter_context(tc.psum_pool(name="ps2", bufs=2))
+        if PIN:
+            ctx.enter_context(tc.manual_schedule())
+
+        raws = {}
+        grps = {}
+        acs = {}
+        tgs = {}
+        banks2 = {}
+
+        def load(n):
+            b, g = divmod(n, 2)
+            raw = rawp.tile([P, 4, I], BF16, tag="raw", name="raw")
+            nc.sync.dma_start(
+                out=raw[:],
+                in_=a_in[b, 512 * g : 512 * (g + 1), :].rearrange("(t p) w -> p t w", p=P),
+            )
+            raws[n] = raw
+
+        mask_sb = const.tile([P, I], BF16, name="mask_sb")
+        nc.sync.dma_start(out=mask_sb[:], in_=mask)
+        w_sb = const.tile([P, C, I], BF16, name="w_sb")
+        for c in range(C):
+            nc.sync.dma_start(out=w_sb[:, c, :], in_=weight[c])
+        for n in range(AHEAD):
+            load(n)
+
+        ident = const.tile([P, P], BF16, name="ident")
+        make_identity(nc, ident[:])
+        identf = const.tile([P, P], F32, name="identf")
+        make_identity(nc, identf[:])
+        noti = const.tile([P, P], BF16, name="noti")
+        nc.vector.tensor_scalar(
+            out=noti[:], in0=ident[:], scalar1=-1.0, scalar2=1.0, op0=ALU.mult, op1=ALU.add
+        )
+
+        comp = const.tile([P, C, I], BF16, name="comp")
+        cg = const.tile([P, 2, C, P, 4], BF16, name="cg", align_bytes=64)
+        ccodes = const.tile([P, 2, C, P], U32, name="ccodes", align_bytes=64)
+        cscales = const.tile([P, 2, C, P], U8, name="cscales", align_bytes=64)
+        rs = const.tile([P, C], F32, name="rs")
+        junk = const.tile([P, I], BF16, name="junk")
+        for c in range(C):
+            nc.vector.tensor_tensor(out=comp[:, c, :], in0=w_sb[:, c, :], in1=mask_sb[:], op=ALU.mult)
+            for g in range(2):
+                xt = ps1.tile([P, 4, P], BF16, tag="s1", name="xt")
+                for t in range(4):
+                    k0 = 512 * g + 128 * t
+                    nc.tensor.transpose(xt[:, t, :], comp[:, c, k0 : k0 + 128], ident[:])
+                nc.vector.tensor_copy(out=cg[:, g, c, :, :], in_=xt[:].rearrange("p t o -> p o t"))
+        nc.vector.quantize_mx(
+            out=ccodes[:].rearrange("p g c o -> p (g c o)").bitcast(FP8X4),
+            scales=cscales[:].rearrange("p g c o -> p (g c o)"),
+            in_=cg[:].rearrange("p g c o t -> p (g c o t)"),
+        )
+        for c in range(C):
+            nc.scalar.activation(out=junk[:], in_=comp[:, c, :], func=ACT.Copy, accum_out=rs[:, c : c + 1])
+
+        inv = const.tile([P, C, P], F32, name="inv")
+
+        def make_inv():
+            ne = const.tile([P, C], F32, name="ne")
+            nc.vector.tensor_scalar(out=ne[:], in0=rs[:], scalar1=0.0, scalar2=1.0, op0=ALU.not_equal, op1=ALU.mult)
+            eq = const.tile([P, C], F32, name="eq")
+            nc.vector.tensor_scalar(out=eq[:], in0=rs[:], scalar1=0.0, scalar2=1.0, op0=ALU.is_equal, op1=ALU.mult)
+            safe = const.tile([P, C], F32, name="safe")
+            nc.vector.tensor_tensor(out=safe[:], in0=rs[:], in1=eq[:], op=ALU.add)
+            rec = const.tile([P, C], F32, name="rec")
+            nc.vector.reciprocal(out=rec[:], in_=safe[:])
+            rp = const.tile([P, C], F32, name="rp")
+            nc.vector.tensor_tensor(out=rp[:], in0=rec[:], in1=ne[:], op=ALU.mult)
+            spread = const.tile([P, C, P], F32, name="spread")
+            nc.vector.tensor_copy(out=spread[:], in_=rp[:].unsqueeze(2).to_broadcast([P, C, P]))
+            rb = ps2.tile([P, C, P], F32, tag="s2", name="rb")
+            for c in range(C):
+                nc.tensor.transpose(rb[:, c, :], spread[:, c, :], identf[:])
+            prod = const.tile([P, C, P], F32, name="prod")
+            nc.vector.tensor_tensor(
+                out=prod[:], in0=rb[:], in1=rp[:].unsqueeze(2).to_broadcast([P, C, P]), op=ALU.mult
+            )
+            nc.vector.scalar_tensor_tensor(
+                out=inv[:].rearrange("p c o -> p (c o)"),
+                in0=prod[:].rearrange("p c o -> p (c o)"),
+                scalar=0.0,
+                in1=prod[:].rearrange("p c o -> p (c o)"),
+                op0=ALU.is_equal,
+                op1=ALU.add,
+            )
+
+        def vrange(n):
+            return (0, VCOLS) if n % 2 == 0 else (I - VCOLS, I)
+
+        def srange(n, piece):
+            s0 = VCOLS if n % 2 == 0 else 0
+            half = (I - VCOLS) // 2
+            return (s0 + piece * half, s0 + (piece + 1) * half)
+
+        def regroup(fn, n, w0, w1):
+            fn(
+                out=grps[n][:, w0:w1, :].rearrange("p (c i) t -> p c t i", i=4),
+                in_=raws[n][:, :, w0:w1].rearrange("p t (c i) -> p c t i", i=4),
+            )
+
+        def front_v(n):
+            g = n % 2
+            diag = raws[n][:].rearrange("p t (j w) -> p (t j) w", w=P)[:, 4 * g : 4 * g + 28 : 9, :]
+            nc.vector.tensor_tensor(
+                out=diag, in0=diag, in1=noti[:].unsqueeze(1).to_broadcast([P, 4, P]), op=ALU.mult
+            )
+            grps[n] = grpp.tile([P, I, 4], BF16, tag="grp", name="grp", align_bytes=64)
+            w0, w1 = vrange(n)
+            regroup(nc.vector.tensor_copy, n, w0, w1)
+
+        def front_s(n, piece):
+            w0, w1 = srange(n, piece)
+            regroup(nc.scalar.copy, n, w0, w1)
+
+        def quant_a(n):
+            codes = acp.tile([P, I], U32, tag="ac", name="ac", align_bytes=64)
+            scl = acp.tile([P, I], U8, tag="asc", name="asc", align_bytes=64)
+            nc.vector.quantize_mx(
+                out=codes[:].bitcast(FP8X4), scales=scl[:], in_=grps[n][:].rearrange("p w t -> p (w t)")
+            )
+            acs[n] = (codes, scl)
+
+        def stage1(b, k):
+            c, gj = divmod(k, 2)
+            if k == 0:
+                tgs[b] = (
+                    tgp.tile([P, C, 2, P, 4], BF16, tag="tg", name="tg", align_bytes=64),
+                    tgp.tile([P, C, 2, P], U32, tag="tcod", name="tcod", align_bytes=64),
+                    tgp.tile([P, C, 2, P], U8, tag="tscl", name="tscl", align_bytes=64),
+                )
+            bank = ps1.tile([P, 4, P], F32, tag="s1", name="bank")
+            for t in range(4):
+                j0 = 512 * gj + 128 * t
+                for g in range(2):
+                    codes, scl = acs[2 * b + g]
+                    nc.tensor.matmul_mx(
+                        out=bank[:, t, :],
+                        lhsT=codes[:, j0 : j0 + 128].bitcast(FP8X4),
+                        lhsT_scale=scl[:, j0 : j0 + 128],
+                        rhs=ccodes[:, g, c, :].bitcast(FP8X4),
+                        rhs_scale=cscales[:, g, c, :],
+                        start=(g == 0),
+                        stop=(g == 1),
+                    )
+            nc.scalar.copy(out=tgs[b][0][:, c, gj, :, :], in_=bank[:].rearrange("p t o -> p o t"))
+
+        def quant_t(b, c):
+            tg, tcod, tscl = tgs[b]
+            nc.vector.quantize_mx(
+                out=tcod[:, c, :, :].rearrange("p g o -> p (g o)").bitcast(FP8X4),
+                scales=tscl[:, c, :, :].rearrange("p g o -> p (g o)"),
+                in_=tg[:, c, :, :, :].rearrange("p g o t -> p (g o t)"),
+            )
+
+        def stage2(b, c):
+            tg, tcod, tscl = tgs[b]
+            if c == 0:
+                banks2[b] = ps2.tile([P, C, P], F32, tag="s2", name="bank2")
+            for gj in range(2):
+                nc.tensor.matmul_mx(
+                    out=banks2[b][:, c, :],
+                    lhsT=tcod[:, c, gj, :].bitcast(FP8X4),
+                    lhsT_scale=tscl[:, c, gj, :],
+                    rhs=ccodes[:, gj, c, :].bitcast(FP8X4),
+                    rhs_scale=cscales[:, gj, c, :],
+                    start=(gj == 0),
+                    stop=(gj == 1),
+                )
+
+        def final(b):
+            osb = outp.tile([P, C, P], F32, tag="osb", name="osb")
+            nc.vector.tensor_tensor(out=osb[:], in0=banks2[b][:], in1=inv[:], op=ALU.mult)
+            eng = nc.sync if b == B - 1 else nc.gpsimd
+            eng.dma_start(out=out[C * b : C * (b + 1)].rearrange("c o q -> o c q"), in_=osb[:])
+
+        for n in range(NCH + 4):
+            odd = n % 2 == 1
+            be = (n - 3) // 2 if odd else (n - 4) // 2
+            k0 = 0 if odd else 4
+            have = 0 <= be < B
+            if n < NCH:
+                front_v(n)
+            if n == 2:
+                make_inv()
+            if odd and 0 <= be - 1 < B:
+                quant_t(be - 1, 3)
+            if (not odd) and have:
+                quant_t(be, 1)
+            if n < NCH:
+                front_s(n, 0)
+            if have:
+                stage1(be, k0)
+                stage1(be, k0 + 1)
+            if odd and 0 <= be - 1 < B:
+                stage2(be - 1, 3)
+            if (not odd) and have:
+                stage2(be, 1)
+            if 1 <= n <= NCH:
+                quant_a(n - 1)
+            if odd and 0 <= be - 1 < B:
+                final(be - 1)
+            if have:
+                quant_t(be, 0 if odd else 2)
+            if n < NCH:
+                front_s(n, 1)
+            if have:
+                stage1(be, k0 + 2)
+                stage1(be, k0 + 3)
+                stage2(be, 0 if odd else 2)
+            if n + AHEAD < NCH:
+                load(n + AHEAD)

@@ -9,26 +9,30 @@ U32 = mybir.dt.uint32
 U8 = mybir.dt.uint8
 FP8X4 = mybir.dt.float8_e4m3fn_x4
 ALU = mybir.AluOpType
-ACT = mybir.ActivationFunctionType
 
 P = 128
 B, I, O, C = 8, 1024, 128, 4
+H = I // 2
 NCH = 2 * B
 FLOPS = 2 * B * C * O * I * I + 2 * B * C * O * I * O
 
 PIN = False
-VCOLS = 640
-AHEAD = 6
+SCOLS = [448,448,384,384,384,384,384,384,384,384,384,384,384,384,384,384]
+RAWB = 4
+TQ_LAG = 3
+F_LAG = 6
+ST_ENG = "sync"
 
 
 def tile_verticalcompression_t_kernel(tc, a_in, mask, weight, out):
     nc = tc.nc
     with ExitStack() as ctx:
         const = ctx.enter_context(tc.tile_pool(name="const", bufs=1))
-        rawp = ctx.enter_context(tc.tile_pool(name="rawp", bufs=AHEAD))
+        rawp = ctx.enter_context(tc.tile_pool(name="rawp", bufs=RAWB))
         grpp = ctx.enter_context(tc.tile_pool(name="grpp", bufs=4))
-        acp = ctx.enter_context(tc.tile_pool(name="acp", bufs=6))
-        tgp = ctx.enter_context(tc.tile_pool(name="tgp", bufs=2))
+        acp = ctx.enter_context(tc.tile_pool(name="acp", bufs=4))
+        tgp = ctx.enter_context(tc.tile_pool(name="tgp", bufs=3))
+        tcp = ctx.enter_context(tc.tile_pool(name="tcp", bufs=6))
         outp = ctx.enter_context(tc.tile_pool(name="outp", bufs=3))
         ps1 = ctx.enter_context(tc.psum_pool(name="ps1", bufs=6))
         ps2 = ctx.enter_context(tc.psum_pool(name="ps2", bufs=2))
@@ -38,25 +42,33 @@ def tile_verticalcompression_t_kernel(tc, a_in, mask, weight, out):
         raws = {}
         grps = {}
         acs = {}
+        banks = {}
         tgs = {}
+        tcs = {}
         banks2 = {}
 
-        def load(n):
-            b, g = divmod(n, 2)
-            raw = rawp.tile([P, 4, I], BF16, tag="raw", name="raw")
-            nc.sync.dma_start(
-                out=raw[:],
-                in_=a_in[b, 512 * g : 512 * (g + 1), :].rearrange("(t p) w -> p t w", p=P),
-            )
-            raws[n] = raw
+        def load(b):
+            raw = rawp.tile([P, 8, I], BF16, tag="raw", name="raw")
+            raws[b] = raw
+            for h in range(2):
+                if b == 0:
+                    nc.sync.dma_start(
+                        out=raw[:, :, H * h : H * (h + 1)],
+                        in_=a_in[b, :, H * h : H * (h + 1)].rearrange("(t p) w -> p t w", p=P),
+                    )
+                else:
+                    nc.sync.dma_start(
+                        out=raw[:, 4 * h : 4 * (h + 1), :],
+                        in_=a_in[b, H * h : H * (h + 1), :].rearrange("(t p) w -> p t w", p=P),
+                    )
 
         mask_sb = const.tile([P, I], BF16, name="mask_sb")
         nc.sync.dma_start(out=mask_sb[:], in_=mask)
         w_sb = const.tile([P, C, I], BF16, name="w_sb")
         for c in range(C):
             nc.sync.dma_start(out=w_sb[:, c, :], in_=weight[c])
-        for n in range(AHEAD):
-            load(n)
+        for b in range(RAWB):
+            load(b)
 
         ident = const.tile([P, P], BF16, name="ident")
         make_identity(nc, ident[:])
@@ -72,26 +84,41 @@ def tile_verticalcompression_t_kernel(tc, a_in, mask, weight, out):
         ccodes = const.tile([P, 2, C, P], U32, name="ccodes", align_bytes=64)
         cscales = const.tile([P, 2, C, P], U8, name="cscales", align_bytes=64)
         rs = const.tile([P, C], F32, name="rs")
-        junk = const.tile([P, I], BF16, name="junk")
+        ones = const.tile([P, 32], BF16, name="ones")
+        nc.gpsimd.memset(ones[:], 1.0)
+        rsbs = {}
+        inv = const.tile([P, C, P], F32, name="inv")
         for c in range(C):
             nc.vector.tensor_tensor(out=comp[:, c, :], in0=w_sb[:, c, :], in1=mask_sb[:], op=ALU.mult)
+        for c in range(C):
             for g in range(2):
                 xt = ps1.tile([P, 4, P], BF16, tag="s1", name="xt")
                 for t in range(4):
-                    k0 = 512 * g + 128 * t
-                    nc.tensor.transpose(xt[:, t, :], comp[:, c, k0 : k0 + 128], ident[:])
-                nc.vector.tensor_copy(out=cg[:, g, c, :, :], in_=xt[:].rearrange("p t o -> p o t"))
-        nc.vector.quantize_mx(
-            out=ccodes[:].rearrange("p g c o -> p (g c o)").bitcast(FP8X4),
-            scales=cscales[:].rearrange("p g c o -> p (g c o)"),
-            in_=cg[:].rearrange("p g c o t -> p (g c o t)"),
-        )
-        for c in range(C):
-            nc.scalar.activation(out=junk[:], in_=comp[:, c, :], func=ACT.Copy, accum_out=rs[:, c : c + 1])
+                    k0 = H * g + P * t
+                    nc.tensor.transpose(xt[:, t, :], comp[:, c, k0 : k0 + P], ident[:])
+                nc.scalar.copy(out=cg[:, g, c, :, :], in_=xt[:].rearrange("p t o -> p o t"))
 
-        inv = const.tile([P, C, P], F32, name="inv")
+        def quant_comp():
+            nc.vector.quantize_mx(
+                out=ccodes[:].rearrange("p g c o -> p (g c o)").bitcast(FP8X4),
+                scales=cscales[:].rearrange("p g c o -> p (g c o)"),
+                in_=cg[:].rearrange("p g c o t -> p (g c o t)"),
+            )
+
+        def row_mass(c):
+            if c == 0:
+                rsbs[0] = ps2.tile([P, C, 32], F32, tag="s2", name="rsb")
+            for i in range(8):
+                nc.tensor.matmul(
+                    out=rsbs[0][:, c, :],
+                    lhsT=cg[:, i // 4, c, :, i % 4],
+                    rhs=ones[:],
+                    start=(i == 0),
+                    stop=(i == 7),
+                )
 
         def make_inv():
+            nc.vector.tensor_copy(out=rs[:], in_=rsbs[0][:, :, 0])
             ne = const.tile([P, C], F32, name="ne")
             nc.vector.tensor_scalar(out=ne[:], in0=rs[:], scalar1=0.0, scalar2=1.0, op0=ALU.not_equal, op1=ALU.mult)
             eq = const.tile([P, C], F32, name="eq")
@@ -120,128 +147,157 @@ def tile_verticalcompression_t_kernel(tc, a_in, mask, weight, out):
                 op1=ALU.add,
             )
 
-        def vrange(n):
-            return (0, VCOLS) if n % 2 == 0 else (I - VCOLS, I)
+        def zero_diag(b, t0, t1):
+            blocks = raws[b][:].rearrange("p t (j w) -> p (t j) w", w=P)[:, 9 * t0 : 9 * (t1 - 1) + 1 : 9, :]
+            nc.vector.tensor_tensor(
+                out=blocks, in0=blocks, in1=noti[:].unsqueeze(1).to_broadcast([P, t1 - t0, P]), op=ALU.mult
+            )
 
-        def srange(n, piece):
-            s0 = VCOLS if n % 2 == 0 else 0
-            half = (I - VCOLS) // 2
-            return (s0 + piece * half, s0 + (piece + 1) * half)
-
-        def regroup(fn, n, w0, w1):
+        def regroup(fn, n, g, w0, w1):
+            b, gj = divmod(n, 2)
             fn(
-                out=grps[n][:, w0:w1, :].rearrange("p (c i) t -> p c t i", i=4),
-                in_=raws[n][:, :, w0:w1].rearrange("p t (c i) -> p c t i", i=4),
+                out=grps[n][:, g, w0:w1, :].rearrange("p (c i) t -> p c t i", i=4),
+                in_=raws[b][:, 4 * g : 4 * (g + 1), H * gj + w0 : H * gj + w1].rearrange(
+                    "p t (c i) -> p c t i", i=4
+                ),
             )
 
         def front_v(n):
-            g = n % 2
-            diag = raws[n][:].rearrange("p t (j w) -> p (t j) w", w=P)[:, 4 * g : 4 * g + 28 : 9, :]
-            nc.vector.tensor_tensor(
-                out=diag, in0=diag, in1=noti[:].unsqueeze(1).to_broadcast([P, 4, P]), op=ALU.mult
-            )
-            grps[n] = grpp.tile([P, I, 4], BF16, tag="grp", name="grp", align_bytes=64)
-            w0, w1 = vrange(n)
-            regroup(nc.vector.tensor_copy, n, w0, w1)
+            b, gj = divmod(n, 2)
+            if b == 0:
+                zero_diag(b, 4 * gj, 4 * gj + 4)
+            elif gj == 0:
+                zero_diag(b, 0, 8)
+            grps[n] = grpp.tile([P, 2, H, 4], BF16, tag="grp", name="grp", align_bytes=64)
+            regroup(nc.vector.tensor_copy, n, gj, 0, H)
+            if SCOLS[n] < H:
+                regroup(nc.vector.tensor_copy, n, 1 - gj, 0, H - SCOLS[n])
 
         def front_s(n, piece):
-            w0, w1 = srange(n, piece)
-            regroup(nc.scalar.copy, n, w0, w1)
+            gj = n % 2
+            half = SCOLS[n] // 2
+            w0 = H - SCOLS[n] + piece * half
+            regroup(nc.scalar.copy, n, 1 - gj, w0, w0 + half)
 
         def quant_a(n):
-            codes = acp.tile([P, I], U32, tag="ac", name="ac", align_bytes=64)
-            scl = acp.tile([P, I], U8, tag="asc", name="asc", align_bytes=64)
+            codes = acp.tile([P, 2, H], U32, tag="ac", name="ac", align_bytes=64)
+            scl = acp.tile([P, 2, H], U8, tag="asc", name="asc", align_bytes=64)
             nc.vector.quantize_mx(
-                out=codes[:].bitcast(FP8X4), scales=scl[:], in_=grps[n][:].rearrange("p w t -> p (w t)")
+                out=codes[:].rearrange("p g w -> p (g w)").bitcast(FP8X4),
+                scales=scl[:].rearrange("p g w -> p (g w)"),
+                in_=grps[n][:].rearrange("p g w t -> p (g w t)"),
             )
             acs[n] = (codes, scl)
 
-        def stage1(b, k):
-            c, gj = divmod(k, 2)
-            if k == 0:
-                tgs[b] = (
-                    tgp.tile([P, C, 2, P, 4], BF16, tag="tg", name="tg", align_bytes=64),
-                    tgp.tile([P, C, 2, P], U32, tag="tcod", name="tcod", align_bytes=64),
-                    tgp.tile([P, C, 2, P], U8, tag="tscl", name="tscl", align_bytes=64),
-                )
+        def stage1(n, c):
+            codes, scl = acs[n]
             bank = ps1.tile([P, 4, P], F32, tag="s1", name="bank")
             for t in range(4):
-                j0 = 512 * gj + 128 * t
                 for g in range(2):
-                    codes, scl = acs[2 * b + g]
                     nc.tensor.matmul_mx(
                         out=bank[:, t, :],
-                        lhsT=codes[:, j0 : j0 + 128].bitcast(FP8X4),
-                        lhsT_scale=scl[:, j0 : j0 + 128],
+                        lhsT=codes[:, g, P * t : P * (t + 1)].bitcast(FP8X4),
+                        lhsT_scale=scl[:, g, P * t : P * (t + 1)],
                         rhs=ccodes[:, g, c, :].bitcast(FP8X4),
                         rhs_scale=cscales[:, g, c, :],
                         start=(g == 0),
                         stop=(g == 1),
                     )
-            nc.scalar.copy(out=tgs[b][0][:, c, gj, :, :], in_=bank[:].rearrange("p t o -> p o t"))
+            banks[(n, c)] = bank
 
-        def quant_t(b, c):
-            tg, tcod, tscl = tgs[b]
+        def evac(fn, n, c):
+            if c == 0:
+                tgs[n] = tgp.tile([P, C, P, 4], BF16, tag="tg", name="tg", align_bytes=64)
+            fn(out=tgs[n][:, c, :, :], in_=banks[(n, c)][:].rearrange("p t o -> p o t"))
+
+        def quant_t(n, c0, c1):
+            if c0 == 0:
+                tcs[n] = (
+                    tcp.tile([P, C, P], U32, tag="tcod", name="tcod", align_bytes=64),
+                    tcp.tile([P, C, P], U8, tag="tscl", name="tscl", align_bytes=64),
+                )
+            tcod, tscl = tcs[n]
             nc.vector.quantize_mx(
-                out=tcod[:, c, :, :].rearrange("p g o -> p (g o)").bitcast(FP8X4),
-                scales=tscl[:, c, :, :].rearrange("p g o -> p (g o)"),
-                in_=tg[:, c, :, :, :].rearrange("p g o t -> p (g o t)"),
+                out=tcod[:, c0:c1, :].rearrange("p c o -> p (c o)").bitcast(FP8X4),
+                scales=tscl[:, c0:c1, :].rearrange("p c o -> p (c o)"),
+                in_=tgs[n][:, c0:c1, :, :].rearrange("p c o t -> p (c o t)"),
             )
 
-        def stage2(b, c):
-            tg, tcod, tscl = tgs[b]
-            if c == 0:
+        def stage2(b, c0, c1):
+            if c0 == 0:
                 banks2[b] = ps2.tile([P, C, P], F32, tag="s2", name="bank2")
-            for gj in range(2):
-                nc.tensor.matmul_mx(
-                    out=banks2[b][:, c, :],
-                    lhsT=tcod[:, c, gj, :].bitcast(FP8X4),
-                    lhsT_scale=tscl[:, c, gj, :],
-                    rhs=ccodes[:, gj, c, :].bitcast(FP8X4),
-                    rhs_scale=cscales[:, gj, c, :],
-                    start=(gj == 0),
-                    stop=(gj == 1),
-                )
+            for c in range(c0, c1):
+                for gj in range(2):
+                    tcod, tscl = tcs[2 * b + gj]
+                    nc.tensor.matmul_mx(
+                        out=banks2[b][:, c, :],
+                        lhsT=tcod[:, c, :].bitcast(FP8X4),
+                        lhsT_scale=tscl[:, c, :],
+                        rhs=ccodes[:, gj, c, :].bitcast(FP8X4),
+                        rhs_scale=cscales[:, gj, c, :],
+                        start=(gj == 0),
+                        stop=(gj == 1),
+                    )
 
-        def final(b):
-            osb = outp.tile([P, C, P], F32, tag="osb", name="osb")
-            nc.vector.tensor_tensor(out=osb[:], in0=banks2[b][:], in1=inv[:], op=ALU.mult)
-            eng = nc.sync if b == B - 1 else nc.gpsimd
-            eng.dma_start(out=out[C * b : C * (b + 1)].rearrange("c o q -> o c q"), in_=osb[:])
+        def final(b, c0, c1):
+            osb = outp.tile([P, c1 - c0, P], F32, tag="osb", name="osb")
+            nc.vector.tensor_tensor(out=osb[:], in0=banks2[b][:, c0:c1, :], in1=inv[:, c0:c1, :], op=ALU.mult)
+            eng = nc.gpsimd if (ST_ENG == "gpsimd" and b < B - 1) else nc.sync
+            eng.dma_start(out=out[C * b + c0 : C * b + c1].rearrange("c o q -> o c q"), in_=osb[:])
 
-        for n in range(NCH + 4):
-            odd = n % 2 == 1
-            be = (n - 3) // 2 if odd else (n - 4) // 2
-            k0 = 0 if odd else 4
-            have = 0 <= be < B
-            if n < NCH:
-                front_v(n)
-            if n == 2:
+        def ok(n):
+            return 0 <= n < NCH
+
+        for m in range(NCH + 1):
+            if ok(m):
+                front_v(m)
+            if m == 0:
+                quant_comp()
+            if ok(m - 2):
+                for c in range(C):
+                    stage1(m - 2, c)
+            if ok(m):
+                front_s(m, 0)
+            if ok(m - 2):
+                evac(nc.scalar.copy, m - 2, 0)
+                evac(nc.scalar.copy, m - 2, 1)
+            if ok(m):
+                front_s(m, 1)
+            if m in (2, 3):
+                row_mass(2 * m - 4)
+                row_mass(2 * m - 3)
+            if ok(m - 2):
+                evac(nc.scalar.copy, m - 2, 2)
+                evac(nc.scalar.copy, m - 2, 3)
+            if m == 4:
                 make_inv()
-            if odd and 0 <= be - 1 < B:
-                quant_t(be - 1, 3)
-            if (not odd) and have:
-                quant_t(be, 1)
-            if n < NCH:
-                front_s(n, 0)
-            if have:
-                stage1(be, k0)
-                stage1(be, k0 + 1)
-            if odd and 0 <= be - 1 < B:
-                stage2(be - 1, 3)
-            if (not odd) and have:
-                stage2(be, 1)
-            if 1 <= n <= NCH:
-                quant_a(n - 1)
-            if odd and 0 <= be - 1 < B:
-                final(be - 1)
-            if have:
-                quant_t(be, 0 if odd else 2)
-            if n < NCH:
-                front_s(n, 1)
-            if have:
-                stage1(be, k0 + 2)
-                stage1(be, k0 + 3)
-                stage2(be, 0 if odd else 2)
-            if n + AHEAD < NCH:
-                load(n + AHEAD)
+            if ok(m - TQ_LAG):
+                quant_t(m - TQ_LAG, 0, C)
+            if ok(m - 1):
+                quant_a(m - 1)
+            n2 = m - TQ_LAG - 1
+            if ok(n2) and n2 % 2 == 1:
+                stage2(n2 // 2, 0, C)
+            n3 = m - F_LAG
+            if ok(n3) and n3 % 2 == 1:
+                final(n3 // 2, 0, C)
+            if ok(m) and m % 2 == 1 and m // 2 + RAWB < B:
+                load(m // 2 + RAWB)
+
+        last = NCH - 1
+        for c in range(C):
+            stage1(last, c)
+        evac(nc.scalar.copy, last, 0)
+        evac(nc.scalar.copy, last, 2)
+        quant_t(last - 1, 0, C)
+        final(B - 3, 0, C)
+        stage2(B - 2, 0, C)
+        evac(nc.vector.tensor_copy, last, 1)
+        quant_t(last, 0, 2)
+        stage2(B - 1, 0, 2)
+        evac(nc.vector.tensor_copy, last, 3)
+        quant_t(last, 2, C)
+        stage2(B - 1, 2, C)
+        final(B - 2, 0, C)
+        final(B - 1, 0, 2)
+        final(B - 1, 2, C)

@@ -16,11 +16,13 @@ H = I // 2
 NCH = 2 * B
 FLOPS = 2 * B * C * O * I * I + 2 * B * C * O * I * O
 
-PIN = False
-SCOLS = [448,448,384,384,384,384,384,384,384,384,384,384,384,384,384,384]
+PIN = True
+SCOLS = [512,512,512,512,352,352,352,352,352,352,352,352,352,352,320,256]
 RAWB = 4
-TQ_LAG = 3
-F_LAG = 6
+JH = 3
+XE_V = (3, 5, 7)
+TQ_LAG = 4
+F_LAG = 7
 ST_ENG = "sync"
 
 
@@ -31,7 +33,7 @@ def tile_verticalcompression_t_kernel(tc, a_in, mask, weight, out):
         rawp = ctx.enter_context(tc.tile_pool(name="rawp", bufs=RAWB))
         grpp = ctx.enter_context(tc.tile_pool(name="grpp", bufs=4))
         acp = ctx.enter_context(tc.tile_pool(name="acp", bufs=4))
-        tgp = ctx.enter_context(tc.tile_pool(name="tgp", bufs=3))
+        tgp = ctx.enter_context(tc.tile_pool(name="tgp", bufs=4))
         tcp = ctx.enter_context(tc.tile_pool(name="tcp", bufs=6))
         outp = ctx.enter_context(tc.tile_pool(name="outp", bufs=3))
         ps1 = ctx.enter_context(tc.psum_pool(name="ps1", bufs=6))
@@ -51,7 +53,7 @@ def tile_verticalcompression_t_kernel(tc, a_in, mask, weight, out):
             raw = rawp.tile([P, 8, I], BF16, tag="raw", name="raw")
             raws[b] = raw
             for h in range(2):
-                if b == 0:
+                if b < JH:
                     nc.sync.dma_start(
                         out=raw[:, :, H * h : H * (h + 1)],
                         in_=a_in[b, :, H * h : H * (h + 1)].rearrange("(t p) w -> p t w", p=P),
@@ -96,7 +98,8 @@ def tile_verticalcompression_t_kernel(tc, a_in, mask, weight, out):
                 for t in range(4):
                     k0 = H * g + P * t
                     nc.tensor.transpose(xt[:, t, :], comp[:, c, k0 : k0 + P], ident[:])
-                nc.scalar.copy(out=cg[:, g, c, :, :], in_=xt[:].rearrange("p t o -> p o t"))
+                fn = nc.vector.tensor_copy if 2 * c + g in XE_V else nc.scalar.copy
+                fn(out=cg[:, g, c, :, :], in_=xt[:].rearrange("p t o -> p o t"))
 
         def quant_comp():
             nc.vector.quantize_mx(
@@ -117,27 +120,40 @@ def tile_verticalcompression_t_kernel(tc, a_in, mask, weight, out):
                     stop=(i == 7),
                 )
 
-        def make_inv():
+        safe = const.tile([P, C], F32, name="safe")
+        rec = const.tile([P, C], F32, name="rec")
+        rp = const.tile([P, C], F32, name="rp")
+        spread = const.tile([P, C, P], F32, name="spread")
+        prod = const.tile([P, C, P], F32, name="prod")
+
+        def inv_rs():
             nc.vector.tensor_copy(out=rs[:], in_=rsbs[0][:, :, 0])
-            ne = const.tile([P, C], F32, name="ne")
-            nc.vector.tensor_scalar(out=ne[:], in0=rs[:], scalar1=0.0, scalar2=1.0, op0=ALU.not_equal, op1=ALU.mult)
-            eq = const.tile([P, C], F32, name="eq")
-            nc.vector.tensor_scalar(out=eq[:], in0=rs[:], scalar1=0.0, scalar2=1.0, op0=ALU.is_equal, op1=ALU.mult)
-            safe = const.tile([P, C], F32, name="safe")
-            nc.vector.tensor_tensor(out=safe[:], in0=rs[:], in1=eq[:], op=ALU.add)
-            rec = const.tile([P, C], F32, name="rec")
-            nc.vector.reciprocal(out=rec[:], in_=safe[:])
-            rp = const.tile([P, C], F32, name="rp")
-            nc.vector.tensor_tensor(out=rp[:], in0=rec[:], in1=ne[:], op=ALU.mult)
-            spread = const.tile([P, C, P], F32, name="spread")
-            nc.vector.tensor_copy(out=spread[:], in_=rp[:].unsqueeze(2).to_broadcast([P, C, P]))
-            rb = ps2.tile([P, C, P], F32, tag="s2", name="rb")
-            for c in range(C):
-                nc.tensor.transpose(rb[:, c, :], spread[:, c, :], identf[:])
-            prod = const.tile([P, C, P], F32, name="prod")
-            nc.vector.tensor_tensor(
-                out=prod[:], in0=rb[:], in1=rp[:].unsqueeze(2).to_broadcast([P, C, P]), op=ALU.mult
+
+        def inv_safe():
+            nc.vector.scalar_tensor_tensor(
+                out=safe[:], in0=rs[:], scalar=0.0, in1=rs[:], op0=ALU.is_equal, op1=ALU.add
             )
+
+        def inv_rec():
+            nc.vector.reciprocal(out=rec[:], in_=safe[:])
+
+        def inv_rp():
+            nc.vector.scalar_tensor_tensor(
+                out=rp[:], in0=rs[:], scalar=0.0, in1=rec[:], op0=ALU.not_equal, op1=ALU.mult
+            )
+
+        def inv_spread():
+            nc.vector.tensor_copy(out=spread[:], in_=rp[:].unsqueeze(2).to_broadcast([P, C, P]))
+            rsbs[1] = ps2.tile([P, C, P], F32, tag="s2", name="rb")
+            for c in range(C):
+                nc.tensor.transpose(rsbs[1][:, c, :], spread[:, c, :], identf[:])
+
+        def inv_prod():
+            nc.vector.tensor_tensor(
+                out=prod[:], in0=rsbs[1][:], in1=rp[:].unsqueeze(2).to_broadcast([P, C, P]), op=ALU.mult
+            )
+
+        def inv_fix():
             nc.vector.scalar_tensor_tensor(
                 out=inv[:].rearrange("p c o -> p (c o)"),
                 in0=prod[:].rearrange("p c o -> p (c o)"),
@@ -146,6 +162,12 @@ def tile_verticalcompression_t_kernel(tc, a_in, mask, weight, out):
                 op0=ALU.is_equal,
                 op1=ALU.add,
             )
+
+        inv_steps = [inv_rs, inv_safe, inv_rec, inv_rp, inv_spread, inv_prod, inv_fix]
+
+        def inv_step(i):
+            if 0 <= i < len(inv_steps):
+                inv_steps[i]()
 
         def zero_diag(b, t0, t1):
             blocks = raws[b][:].rearrange("p t (j w) -> p (t j) w", w=P)[:, 9 * t0 : 9 * (t1 - 1) + 1 : 9, :]
@@ -162,12 +184,15 @@ def tile_verticalcompression_t_kernel(tc, a_in, mask, weight, out):
                 ),
             )
 
-        def front_v(n):
+        def front_m(n):
             b, gj = divmod(n, 2)
-            if b == 0:
+            if b < JH:
                 zero_diag(b, 4 * gj, 4 * gj + 4)
             elif gj == 0:
                 zero_diag(b, 0, 8)
+
+        def front_v(n):
+            b, gj = divmod(n, 2)
             grps[n] = grpp.tile([P, 2, H, 4], BF16, tag="grp", name="grp", align_bytes=64)
             regroup(nc.vector.tensor_copy, n, gj, 0, H)
             if SCOLS[n] < H:
@@ -248,14 +273,22 @@ def tile_verticalcompression_t_kernel(tc, a_in, mask, weight, out):
         def ok(n):
             return 0 <= n < NCH
 
+        for c in range(C):
+            row_mass(c)
+        front_m(0)
+
         for m in range(NCH + 1):
             if ok(m):
                 front_v(m)
             if m == 0:
                 quant_comp()
+            inv_step(2 * (m - 2))
             if ok(m - 2):
                 for c in range(C):
                     stage1(m - 2, c)
+            if ok(m - 3):
+                evac(nc.scalar.copy, m - 3, 2)
+                evac(nc.scalar.copy, m - 3, 3)
             if ok(m):
                 front_s(m, 0)
             if ok(m - 2):
@@ -263,16 +296,11 @@ def tile_verticalcompression_t_kernel(tc, a_in, mask, weight, out):
                 evac(nc.scalar.copy, m - 2, 1)
             if ok(m):
                 front_s(m, 1)
-            if m in (2, 3):
-                row_mass(2 * m - 4)
-                row_mass(2 * m - 3)
-            if ok(m - 2):
-                evac(nc.scalar.copy, m - 2, 2)
-                evac(nc.scalar.copy, m - 2, 3)
-            if m == 4:
-                make_inv()
             if ok(m - TQ_LAG):
                 quant_t(m - TQ_LAG, 0, C)
+            if ok(m + 1):
+                front_m(m + 1)
+            inv_step(2 * (m - 2) + 1)
             if ok(m - 1):
                 quant_a(m - 1)
             n2 = m - TQ_LAG - 1
@@ -287,11 +315,14 @@ def tile_verticalcompression_t_kernel(tc, a_in, mask, weight, out):
         last = NCH - 1
         for c in range(C):
             stage1(last, c)
+        evac(nc.scalar.copy, last - 1, 2)
+        evac(nc.vector.tensor_copy, last - 1, 3)
         evac(nc.scalar.copy, last, 0)
         evac(nc.scalar.copy, last, 2)
+        quant_t(last - 2, 0, C)
         quant_t(last - 1, 0, C)
-        final(B - 3, 0, C)
         stage2(B - 2, 0, C)
+        final(B - 3, 0, C)
         evac(nc.vector.tensor_copy, last, 1)
         quant_t(last, 0, 2)
         stage2(B - 1, 0, 2)

@@ -16,11 +16,11 @@ H = I // 2
 NCH = 2 * B
 FLOPS = 2 * B * C * O * I * I + 2 * B * C * O * I * O
 
-PIN = True
-SCOLS = [512,512,512,512,352,352,352,352,352,352,352,352,352,352,320,256]
+PIN = False
+SCOLS = [512,512,512,512,416,416,416,416,416,416,416,416,416,416,352,288]
 RAWB = 4
 JH = 3
-XE_V = (3, 5, 7)
+XE_V = (7,)
 TQ_LAG = 4
 F_LAG = 7
 ST_ENG = "sync"

@@ -22,7 +22,7 @@ RAWB = 4
 JH = 3
 XE_V = (7,)
 TQ_LAG = 4
-F_LAG = 7
+F_LAG = 5
 ST_ENG = "sync"
 
 
@@ -36,8 +36,8 @@ def tile_verticalcompression_t_kernel(tc, a_in, mask, weight, out):
         tgp = ctx.enter_context(tc.tile_pool(name="tgp", bufs=4))
         tcp = ctx.enter_context(tc.tile_pool(name="tcp", bufs=6))
         outp = ctx.enter_context(tc.tile_pool(name="outp", bufs=3))
-        ps1 = ctx.enter_context(tc.psum_pool(name="ps1", bufs=6))
-        ps2 = ctx.enter_context(tc.psum_pool(name="ps2", bufs=2))
+        ps1 = ctx.enter_context(tc.psum_pool(name="ps1", bufs=7))
+        ps2 = ctx.enter_context(tc.psum_pool(name="ps2", bufs=1))
         if PIN:
             ctx.enter_context(tc.manual_schedule())
 
@@ -322,13 +322,12 @@ def tile_verticalcompression_t_kernel(tc, a_in, mask, weight, out):
         quant_t(last - 2, 0, C)
         quant_t(last - 1, 0, C)
         stage2(B - 2, 0, C)
-        final(B - 3, 0, C)
+        final(B - 2, 0, C)
         evac(nc.vector.tensor_copy, last, 1)
         quant_t(last, 0, 2)
         stage2(B - 1, 0, 2)
         evac(nc.vector.tensor_copy, last, 3)
         quant_t(last, 2, C)
         stage2(B - 1, 2, C)
-        final(B - 2, 0, C)
         final(B - 1, 0, 2)
         final(B - 1, 2, C)

@@ -200,9 +200,8 @@ def tile_verticalcompression_t_kernel(tc, a_in, mask, weight, out):
 
         def front_s(n, piece):
             gj = n % 2
-            half = SCOLS[n] // 2
-            w0 = H - SCOLS[n] + piece * half
-            regroup(nc.scalar.copy, n, 1 - gj, w0, w0 + half)
+            if piece == 0:
+                regroup(nc.scalar.copy, n, 1 - gj, H - SCOLS[n], H)
 
         def quant_a(n):
             codes = acp.tile([P, 2, H], U32, tag="ac", name="ac", align_bytes=64)

from contextlib import ExitStack

import concourse.mybir as mybir
from concourse.masks import make_identity

F32 = mybir.dt.float32
BF16 = mybir.dt.bfloat16
U32 = mybir.dt.uint32
U8 = mybir.dt.uint8
FP8X4 = mybir.dt.float8_e4m3fn_x4
ALU = mybir.AluOpType

P = 128
B, I, O, C = 8, 1024, 128, 4
H = I // 2
NCH = 2 * B
FLOPS = 2 * B * C * O * I * I + 2 * B * C * O * I * O

PIN = False
SCOLS = [512,512,512,512,416,416,416,416,416,416,416,416,416,416,352,288]
RAWB = 4
JH = 3
XE_V = (7,)
TQ_LAG = 4
F_LAG = 5
ST_ENG = "sync"


def tile_verticalcompression_t_kernel(tc, a_in, mask, weight, out):
    nc = tc.nc
    with ExitStack() as ctx:
        const = ctx.enter_context(tc.tile_pool(name="const", bufs=1))
        rawp = ctx.enter_context(tc.tile_pool(name="rawp", bufs=RAWB))
        grpp = ctx.enter_context(tc.tile_pool(name="grpp", bufs=4))
        acp = ctx.enter_context(tc.tile_pool(name="acp", bufs=4))
        tgp = ctx.enter_context(tc.tile_pool(name="tgp", bufs=4))
        tcp = ctx.enter_context(tc.tile_pool(name="tcp", bufs=6))
        outp = ctx.enter_context(tc.tile_pool(name="outp", bufs=3))
        ps1 = ctx.enter_context(tc.psum_pool(name="ps1", bufs=7))
        ps2 = ctx.enter_context(tc.psum_pool(name="ps2", bufs=1))
        if PIN:
            ctx.enter_context(tc.manual_schedule())

        raws = {}
        grps = {}
        acs = {}
        banks = {}
        tgs = {}
        tcs = {}
        banks2 = {}

        def load(b):
            raw = rawp.tile([P, 8, I], BF16, tag="raw", name="raw")
            raws[b] = raw
            for h in range(2):
                if b < JH:
                    nc.sync.dma_start(
                        out=raw[:, :, H * h : H * (h + 1)],
                        in_=a_in[b, :, H * h : H * (h + 1)].rearrange("(t p) w -> p t w", p=P),
                    )
                else:
                    nc.sync.dma_start(
                        out=raw[:, 4 * h : 4 * (h + 1), :],
                        in_=a_in[b, H * h : H * (h + 1), :].rearrange("(t p) w -> p t w", p=P),
                    )

        mask_sb = const.tile([P, I], BF16, name="mask_sb")
        nc.sync.dma_start(out=mask_sb[:], in_=mask)
        w_sb = const.tile([P, C, I], BF16, name="w_sb")
        for c in range(C):
            nc.sync.dma_start(out=w_sb[:, c, :], in_=weight[c])
        for b in range(RAWB):
            load(b)

        ident = const.tile([P, P], BF16, name="ident")
        make_identity(nc, ident[:])
        identf = const.tile([P, P], F32, name="identf")
        make_identity(nc, identf[:])
        noti = const.tile([P, P], BF16, name="noti")
        nc.vector.tensor_scalar(
            out=noti[:], in0=ident[:], scalar1=-1.0, scalar2=1.0, op0=ALU.mult, op1=ALU.add
        )

        comp = const.tile([P, C, I], BF16, name="comp")
        cg = const.tile([P, 2, C, P, 4], BF16, name="cg", align_bytes=64)
        ccodes = const.tile([P, 2, C, P], U32, name="ccodes", align_bytes=64)
        cscales = const.tile([P, 2, C, P], U8, name="cscales", align_bytes=64)
        rs = const.tile([P, C], F32, name="rs")
        ones = const.tile([P, 32], BF16, name="ones")
        nc.gpsimd.memset(ones[:], 1.0)
        rsbs = {}
        inv = const.tile([P, C, P], F32, name="inv")
        for c in range(C):
            nc.vector.tensor_tensor(out=comp[:, c, :], in0=w_sb[:, c, :], in1=mask_sb[:], op=ALU.mult)
        for c in range(C):
            for g in range(2):
                xt = ps1.tile([P, 4, P], BF16, tag="s1", name="xt")
                for t in range(4):
                    k0 = H * g + P * t
                    nc.tensor.transpose(xt[:, t, :], comp[:, c, k0 : k0 + P], ident[:])
                fn = nc.vector.tensor_copy if 2 * c + g in XE_V else nc.scalar.copy
                fn(out=cg[:, g, c, :, :], in_=xt[:].rearrange("p t o -> p o t"))

        def quant_comp():
            nc.vector.quantize_mx(
                out=ccodes[:].rearrange("p g c o -> p (g c o)").bitcast(FP8X4),
                scales=cscales[:].rearrange("p g c o -> p (g c o)"),
                in_=cg[:].rearrange("p g c o t -> p (g c o t)"),
            )

        def row_mass(c):
            if c == 0:
                rsbs[0] = ps2.tile([P, C, 32], F32, tag="s2", name="rsb")
            for i in range(8):
                nc.tensor.matmul(
                    out=rsbs[0][:, c, :],
                    lhsT=cg[:, i // 4, c, :, i % 4],
                    rhs=ones[:],
                    start=(i == 0),
                    stop=(i == 7),
                )

        safe = const.tile([P, C], F32, name="safe")
        rec = const.tile([P, C], F32, name="rec")
        rp = const.tile([P, C], F32, name="rp")
        spread = const.tile([P, C, P], F32, name="spread")
        prod = const.tile([P, C, P], F32, name="prod")

        def inv_rs():
            nc.vector.tensor_copy(out=rs[:], in_=rsbs[0][:, :, 0])

        def inv_safe():
            nc.vector.scalar_tensor_tensor(
                out=safe[:], in0=rs[:], scalar=0.0, in1=rs[:], op0=ALU.is_equal, op1=ALU.add
            )

        def inv_rec():
            nc.vector.reciprocal(out=rec[:], in_=safe[:])

        def inv_rp():
            nc.vector.scalar_tensor_tensor(
                out=rp[:], in0=rs[:], scalar=0.0, in1=rec[:], op0=ALU.not_equal, op1=ALU.mult
            )

        def inv_spread():
            nc.vector.tensor_copy(out=spread[:], in_=rp[:].unsqueeze(2).to_broadcast([P, C, P]))
            rsbs[1] = ps2.tile([P, C, P], F32, tag="s2", name="rb")
            for c in range(C):
                nc.tensor.transpose(rsbs[1][:, c, :], spread[:, c, :], identf[:])

        def inv_prod():
            nc.vector.tensor_tensor(
                out=prod[:], in0=rsbs[1][:], in1=rp[:].unsqueeze(2).to_broadcast([P, C, P]), op=ALU.mult
            )

        def inv_fix():
            nc.vector.scalar_tensor_tensor(
                out=inv[:].rearrange("p c o -> p (c o)"),
                in0=prod[:].rearrange("p c o -> p (c o)"),
                scalar=0.0,
                in1=prod[:].rearrange("p c o -> p (c o)"),
                op0=ALU.is_equal,
                op1=ALU.add,
            )

        inv_steps = [inv_rs, inv_safe, inv_rec, inv_rp, inv_spread, inv_prod, inv_fix]

        def inv_step(i):
            if 0 <= i < len(inv_steps):
                inv_steps[i]()

        def zero_diag(b, t0, t1):
            blocks = raws[b][:].rearrange("p t (j w) -> p (t j) w", w=P)[:, 9 * t0 : 9 * (t1 - 1) + 1 : 9, :]
            nc.vector.tensor_tensor(
                out=blocks, in0=blocks, in1=noti[:].unsqueeze(1).to_broadcast([P, t1 - t0, P]), op=ALU.mult
            )

        def regroup(fn, n, g, w0, w1):
            b, gj = divmod(n, 2)
            fn(
                out=grps[n][:, g, w0:w1, :].rearrange("p (c i) t -> p c t i", i=4),
                in_=raws[b][:, 4 * g : 4 * (g + 1), H * gj + w0 : H * gj + w1].rearrange(
                    "p t (c i) -> p c t i", i=4
                ),
            )

        def front_m(n):
            b, gj = divmod(n, 2)
            if b < JH:
                zero_diag(b, 4 * gj, 4 * gj + 4)
            elif gj == 0:
                zero_diag(b, 0, 8)

        def front_v(n):
            b, gj = divmod(n, 2)
            grps[n] = grpp.tile([P, 2, H, 4], BF16, tag="grp", name="grp", align_bytes=64)
            regroup(nc.vector.tensor_copy, n, gj, 0, H)
            if SCOLS[n] < H:
                regroup(nc.vector.tensor_copy, n, 1 - gj, 0, H - SCOLS[n])

        def front_s(n, piece):
            gj = n % 2
            if piece == 0:
                regroup(nc.scalar.copy, n, 1 - gj, H - SCOLS[n], H)

        def quant_a(n):
            codes = acp.tile([P, 2, H], U32, tag="ac", name="ac", align_bytes=64)
            scl = acp.tile([P, 2, H], U8, tag="asc", name="asc", align_bytes=64)
            nc.vector.quantize_mx(
                out=codes[:].rearrange("p g w -> p (g w)").bitcast(FP8X4),
                scales=scl[:].rearrange("p g w -> p (g w)"),
                in_=grps[n][:].rearrange("p g w t -> p (g w t)"),
            )
            acs[n] = (codes, scl)

        def stage1(n, c):
            codes, scl = acs[n]
            bank = ps1.tile([P, 4, P], F32, tag="s1", name="bank")
            for t in range(4):
                for g in range(2):
                    nc.tensor.matmul_mx(
                        out=bank[:, t, :],
                        lhsT=codes[:, g, P * t : P * (t + 1)].bitcast(FP8X4),
                        lhsT_scale=scl[:, g, P * t : P * (t + 1)],
                        rhs=ccodes[:, g, c, :].bitcast(FP8X4),
                        rhs_scale=cscales[:, g, c, :],
                        start=(g == 0),
                        stop=(g == 1),
                    )
            banks[(n, c)] = bank

        def evac(fn, n, c):
            if c == 0:
                tgs[n] = tgp.tile([P, C, P, 4], BF16, tag="tg", name="tg", align_bytes=64)
            fn(out=tgs[n][:, c, :, :], in_=banks[(n, c)][:].rearrange("p t o -> p o t"))

        def quant_t(n, c0, c1):
            if c0 == 0:
                tcs[n] = (
                    tcp.tile([P, C, P], U32, tag="tcod", name="tcod", align_bytes=64),
                    tcp.tile([P, C, P], U8, tag="tscl", name="tscl", align_bytes=64),
                )
            tcod, tscl = tcs[n]
            nc.vector.quantize_mx(
                out=tcod[:, c0:c1, :].rearrange("p c o -> p (c o)").bitcast(FP8X4),
                scales=tscl[:, c0:c1, :].rearrange("p c o -> p (c o)"),
                in_=tgs[n][:, c0:c1, :, :].rearrange("p c o t -> p (c o t)"),
            )

        def stage2(b, c0, c1):
            if c0 == 0:
                banks2[b] = ps2.tile([P, C, P], F32, tag="s2", name="bank2")
            for c in range(c0, c1):
                for gj in range(2):
                    tcod, tscl = tcs[2 * b + gj]
                    nc.tensor.matmul_mx(
                        out=banks2[b][:, c, :],
                        lhsT=tcod[:, c, :].bitcast(FP8X4),
                        lhsT_scale=tscl[:, c, :],
                        rhs=ccodes[:, gj, c, :].bitcast(FP8X4),
                        rhs_scale=cscales[:, gj, c, :],
                        start=(gj == 0),
                        stop=(gj == 1),
                    )

        def final(b, c0, c1):
            osb = outp.tile([P, c1 - c0, P], F32, tag="osb", name="osb")
            nc.vector.tensor_tensor(out=osb[:], in0=banks2[b][:, c0:c1, :], in1=inv[:, c0:c1, :], op=ALU.mult)
            eng = nc.gpsimd if (ST_ENG == "gpsimd" and b < B - 1) else nc.sync
            eng.dma_start(out=out[C * b + c0 : C * b + c1].rearrange("c o q -> o c q"), in_=osb[:])

        def ok(n):
            return 0 <= n < NCH

        for c in range(C):
            row_mass(c)
        front_m(0)

        for m in range(NCH + 1):
            if ok(m):
                front_v(m)
            if m == 0:
                quant_comp()
            inv_step(2 * (m - 2))
            if ok(m - 2):
                for c in range(C):
                    stage1(m - 2, c)
            if ok(m - 3):
                evac(nc.scalar.copy, m - 3, 2)
                evac(nc.scalar.copy, m - 3, 3)
            if ok(m):
                front_s(m, 0)
            if ok(m - 2):
                evac(nc.scalar.copy, m - 2, 0)
                evac(nc.scalar.copy, m - 2, 1)
            if ok(m):
                front_s(m, 1)
            if ok(m - TQ_LAG):
                quant_t(m - TQ_LAG, 0, C)
            if ok(m + 1):
                front_m(m + 1)
            inv_step(2 * (m - 2) + 1)
            if ok(m - 1):
                quant_a(m - 1)
            n2 = m - TQ_LAG - 1
            if ok(n2) and n2 % 2 == 1:
                stage2(n2 // 2, 0, C)
            n3 = m - F_LAG
            if ok(n3) and n3 % 2 == 1:
                final(n3 // 2, 0, C)
            if ok(m) and m % 2 == 1 and m // 2 + RAWB < B:
                load(m // 2 + RAWB)

        last = NCH - 1
        for c in range(C):
            stage1(last, c)
        evac(nc.scalar.copy, last - 1, 2)
        evac(nc.vector.tensor_copy, last - 1, 3)
        evac(nc.scalar.copy, last, 0)
        evac(nc.scalar.copy, last, 2)
        quant_t(last - 2, 0, C)
        quant_t(last - 1, 0, C)
        stage2(B - 2, 0, C)
        final(B - 2, 0, C)
        evac(nc.vector.tensor_copy, last, 1)
        quant_t(last, 0, 2)
        stage2(B - 1, 0, 2)
        evac(nc.vector.tensor_copy, last, 3)
        quant_t(last, 2, C)
        stage2(B - 1, 2, C)
        final(B - 1, 0, 2)
        final(B - 1, 2, C)
